import numpy as np
import ml_dtypes

BF16 = ml_dtypes.bfloat16


def bf(x):
    return np.asarray(x, np.float32).astype(BF16)


def f32(x):
    return np.asarray(x, np.float32)


def f64(x):
    return np.asarray(x).astype(np.float64)


def striped(idx):
    return np.tile(idx.reshape(-1, 16).T, (8, 1))


Q, T, C, C3, O, S, N = 8, 256, 512, 1536, 256, 4096, 2048


def sigmoid(v):
    return 1.0 / (1.0 + np.exp(-v))


def setup_inputs():
    return {
        "base": f32(np.random.standard_normal((O, S))),
        "adj_t": bf(np.random.uniform(0.0, 1.0, (Q, T, T)) * 2.0 / np.sqrt(T)),
        "ann": bf(np.random.standard_normal((C, N))),
        "gc_bias": f32(0.3 * np.random.standard_normal((C, 1))),
        "gru_w": bf(np.random.standard_normal((C, C3)) / np.sqrt(C)),
        "gru_u": bf(np.random.standard_normal((C, C3)) / np.sqrt(C)),
        "gru_bx": f32(0.3 * np.random.standard_normal((C3, 1))),
        "gru_bh": f32(0.3 * np.random.standard_normal((C3, 1))),
        "dense_w": bf(np.random.standard_normal((C, O)) / np.sqrt(C)),
        "dense_b": f32(0.1 * np.random.standard_normal((O, 1))),
        "offs": striped(np.random.permutation(S)[:N]),
    }


def reference(base, adj_t, ann, gc_bias, gru_w, gru_u, gru_bx, gru_bh, dense_w, dense_b, offs):
    idx = offs[:16].T.reshape(-1)
    h = f64(ann)
    hq = h.reshape(C, Q, T).transpose(1, 0, 2)
    msg = np.matmul(hq, f64(adj_t)).transpose(1, 0, 2).reshape(C, N) + f64(gc_bias)
    px = f64(gru_w).T @ msg + f64(gru_bx)
    ph = f64(gru_u).T @ h + f64(gru_bh)
    z = sigmoid(px[:C] + ph[:C])
    r = sigmoid(px[C:C + C] + ph[C:C + C])
    cand = np.tanh(px[C + C:] + r * ph[C + C:])
    hnew = z * h + (1.0 - z) * cand
    res = f64(base).copy()
    res[:, idx] = f64(dense_w).T @ hnew + f64(dense_b)
    return res

@@ -1,0 +1,193 @@
+import concourse.mybir as mybir
+from concourse.masks import make_identity
+
+P = 128
+Q, T = 8, 256
+C, O, S = 512, 256, 4096
+N = Q * T
+CB = C // P
+OB = O // P
+W = 512
+CHUNKS = N // W
+GRAPHS = W // T
+UB = T // P
+NB = W // P
+
+FLOPS = 2 * (Q * C * T * T + 2 * C * 3 * C * N + C * O * N)
+
+BF16, F32, U16 = mybir.dt.bfloat16, mybir.dt.float32, mybir.dt.uint16
+ADD, MULT, SUBTRACT = mybir.AluOpType.add, mybir.AluOpType.mult, mybir.AluOpType.subtract
+SIGMOID = mybir.ActivationFunctionType.Sigmoid
+TANH = mybir.ActivationFunctionType.Tanh
+IDENTITY = mybir.ActivationFunctionType.Identity
+
+GC_COL = 0
+BX_COL = GC_COL + CB
+BH_COL = BX_COL + 3 * CB
+DB_COL = BH_COL + 3 * CB
+BIAS_COLS = DB_COL + OB
+
+
+def tile_gatedgraphconvolution_b_kernel(
+    tc, base, adj_t, ann, gc_bias, gru_w, gru_u, gru_bx, gru_bh, dense_w, dense_b, offs, out
+):
+    nc = tc.nc
+    with (
+        tc.tile_pool(name="held", bufs=1) as held,
+        tc.tile_pool(name="work", bufs=3) as work,
+        tc.psum_pool(name="psum", bufs=8) as psum,
+    ):
+        offsets = held.tile([P, N // 16], U16, name="offsets")
+        nc.sync.dma_start(offsets[:], offs)
+
+        bias_rows = held.tile([P, P], F32, name="bias_rows")
+        nc.vector.memset(bias_rows[:], 0.0)
+        for vector, col, blocks in (
+            (gc_bias, GC_COL, CB),
+            (gru_bx, BX_COL, 3 * CB),
+            (gru_bh, BH_COL, 3 * CB),
+            (dense_b, DB_COL, OB),
+        ):
+            nc.scalar.dma_start(bias_rows[col : col + blocks, :], vector.rearrange("(k p) one -> k (p one)", p=P))
+
+        ann_sb = held.tile([P, CB, N], BF16, name="ann_sb")
+        adj_sb = held.tile([P, Q * UB, T], BF16, name="adj_sb")
+        ann_blocks = ann.rearrange("(k p) n -> p k n", p=P)
+        adj_blocks = adj_t.flatten_outer_dims().rearrange("(b p) t -> p b t", p=P)
+        for n in range(CHUNKS):
+            nc.sync.dma_start(ann_sb[:, :, n * W : (n + 1) * W], ann_blocks[:, :, n * W : (n + 1) * W])
+            nc.scalar.dma_start(adj_sb[:, n * NB : (n + 1) * NB, :], adj_blocks[:, n * NB : (n + 1) * NB, :])
+
+        gru_u_sb = held.tile([P, CB, 3 * C], BF16, name="gru_u_sb")
+        gru_w_sb = held.tile([P, CB, 3 * C], BF16, name="gru_w_sb")
+        dense_w_sb = held.tile([P, CB, O], BF16, name="dense_w_sb")
+        nc.sync.dma_start(gru_u_sb[:], gru_u.rearrange("(k p) m -> p k m", p=P))
+        nc.scalar.dma_start(gru_w_sb[:], gru_w.rearrange("(k p) m -> p k m", p=P))
+        nc.scalar.dma_start(dense_w_sb[:], dense_w.rearrange("(k p) m -> p k m", p=P))
+
+        windows = [held.tile([P, S], F32, name=f"window{o}") for o in range(OB)]
+        nc.sync.dma_start(windows[0][:], base[0:P, :])
+        nc.scalar.dma_start(windows[1][:], base[P : 2 * P, :])
+
+        ident_bf = held.tile([P, P], BF16, name="ident_bf")
+        make_identity(nc, ident_bf[:])
+        ident_f32 = held.tile([P, P], F32, name="ident_f32")
+        nc.vector.tensor_copy(ident_f32[:], ident_bf[:])
+
+        ann_t_sb = held.tile([P, N // P, C], BF16, name="ann_t_sb")
+        msg_sb = held.tile([P, CB, N], BF16, name="msg_sb")
+        hnew_sb = held.tile([P, CB, N], BF16, name="hnew_sb")
+        y_sb = [held.tile([P, N], F32, name=f"y_sb{o}") for o in range(OB)]
+        bias_sb = held.tile([P, BIAS_COLS], F32, name="bias_sb")
+        gate_bias = held.tile([P, 2 * CB], F32, name="gate_bias")
+        dense_b_wide = [held.tile([P, N], F32, name=f"dense_b_wide{o}") for o in range(OB)]
+
+        def transpose_ann(n):
+            for b in range(n * NB, (n + 1) * NB):
+                flipped = psum.tile([P, C], BF16, name="flipped", tag="bank")
+                for k in range(CB):
+                    nc.tensor.transpose(flipped[:, k * P : (k + 1) * P], ann_sb[:, k, b * P : (b + 1) * P], ident_bf[:])
+                nc.vector.tensor_copy(ann_t_sb[:, b, :], flipped[:])
+
+        def make_biases():
+            columns = psum.tile([P, P], F32, name="columns", tag="bank")
+            nc.tensor.transpose(columns[:], bias_rows[:], ident_f32[:])
+            nc.vector.tensor_copy(bias_sb[:], columns[:, 0:BIAS_COLS])
+            nc.vector.tensor_tensor(
+                gate_bias[:], bias_sb[:, BX_COL : BX_COL + 2 * CB], bias_sb[:, BH_COL : BH_COL + 2 * CB], ADD
+            )
+
+        def adjacency(n):
+            for k in range(CB):
+                msg_ps = psum.tile([P, W], F32, name="msg_ps", tag="bank")
+                for g in range(GRAPHS):
+                    for u in range(UB):
+                        b = (n * GRAPHS + g) * UB + u
+                        nc.tensor.matmul(
+                            msg_ps[:, g * T : (g + 1) * T],
+                            ann_t_sb[:, b, k * P : (k + 1) * P],
+                            adj_sb[:, b, :],
+                            start=(u == 0),
+                            stop=(u == UB - 1),
+                        )
+                nc.scalar.activation(
+                    msg_sb[:, k, n * W : (n + 1) * W], msg_ps[:], IDENTITY, bias=bias_sb[:, GC_COL + k : GC_COL + k + 1]
+                )
+
+        def product(bank, terms, m, n):
+            last = len(terms) * CB - 1
+            for i, (weights, moving) in enumerate(terms):
+                for k in range(CB):
+                    nc.tensor.matmul(
+                        bank[:],
+                        weights[:, k, m * P : (m + 1) * P],
+                        moving[:, k, n * W : (n + 1) * W],
+                        start=(i * CB + k == 0),
+                        stop=(i * CB + k == last),
+                    )
+
+        def gru(n, k):
+            state = ann_sb[:, k, n * W : (n + 1) * W]
+            from_state, from_msg = (gru_u_sb, ann_sb), (gru_w_sb, msg_sb)
+
+            r_ps = psum.tile([P, W], F32, name="r_ps", tag="bank")
+            product(r_ps, (from_state, from_msg), CB + k, n)
+            r = work.tile([P, W], F32, name="r")
+            nc.scalar.activation(r[:], r_ps[:], SIGMOID, bias=gate_bias[:, CB + k : CB + k + 1])
+
+            ph_ps = psum.tile([P, W], F32, name="ph_ps", tag="bank")
+            product(ph_ps, (from_state,), 2 * CB + k, n)
+            gated = work.tile([P, W], F32, name="gated")
+            bh_col = BH_COL + 2 * CB + k
+            nc.vector.scalar_tensor_tensor(gated[:], ph_ps[:], bias_sb[:, bh_col : bh_col + 1], r[:], ADD, MULT)
+
+            px_ps = psum.tile([P, W], F32, name="px_ps", tag="bank")
+            product(px_ps, (from_msg,), 2 * CB + k, n)
+            pre = work.tile([P, W], F32, name="pre")
+            nc.vector.tensor_tensor(pre[:], gated[:], px_ps[:], ADD)
+            cand = work.tile([P, W], F32, name="cand")
+            bx_col = BX_COL + 2 * CB + k
+            nc.scalar.activation(cand[:], pre[:], TANH, bias=bias_sb[:, bx_col : bx_col + 1])
+
+            z_ps = psum.tile([P, W], F32, name="z_ps", tag="bank")
+            product(z_ps, (from_state, from_msg), k, n)
+            z = work.tile([P, W], F32, name="z")
+            nc.scalar.activation(z[:], z_ps[:], SIGMOID, bias=gate_bias[:, k : k + 1])
+
+            diff = work.tile([P, W], F32, name="diff")
+            nc.vector.tensor_tensor(diff[:], state, cand[:], SUBTRACT)
+            kept = work.tile([P, W], F32, name="kept")
+            nc.vector.tensor_tensor(kept[:], z[:], diff[:], MULT)
+            nc.vector.tensor_tensor(hnew_sb[:, k, n * W : (n + 1) * W], kept[:], cand[:], ADD)
+
+        def dense(n):
+            for o in range(OB):
+                y_ps = psum.tile([P, W], F32, name="y_ps", tag="bank")
+                product(y_ps, ((dense_w_sb, hnew_sb),), o, n)
+                nc.scalar.copy(y_sb[o][:, n * W : (n + 1) * W], y_ps[:])
+
+        transpose_ann(0)
+        make_biases()
+        for n in range(CHUNKS):
+            if n + 1 < CHUNKS:
+                transpose_ann(n + 1)
+            adjacency(n)
+
+        for o in range(OB):
+            nc.vector.tensor_copy(dense_b_wide[o][:], bias_sb[:, DB_COL + o : DB_COL + o + 1].to_broadcast([P, N]))
+
+        for n in range(CHUNKS):
+            for k in range(CB):
+                gru(n, k)
+                if k == 0 and n > 0:
+                    dense(n - 1)
+        dense(CHUNKS - 1)
+
+        for o in range(OB):
+            nc.vector.tensor_tensor(
+                windows[o][:].indirect(offsets[:]),
+                y_sb[o][:],
+                dense_b_wide[o][:],
+                ADD,
+            )
+            nc.sync.dma_start(out[o * P : (o + 1) * P, :], windows[o][:])

@@ -160,11 +160,10 @@ def tile_gatedgraphconvolution_b_kernel(
             nc.vector.tensor_tensor(kept[:], z[:], diff[:], MULT)
             nc.vector.tensor_tensor(hnew_sb[:, k, n * W : (n + 1) * W], kept[:], cand[:], ADD)
 
-        def dense(n):
-            for o in range(OB):
-                y_ps = psum.tile([P, W], F32, name="y_ps", tag="bank")
-                product(y_ps, ((dense_w_sb, hnew_sb),), o, n)
-                nc.scalar.copy(y_sb[o][:, n * W : (n + 1) * W], y_ps[:])
+        def dense(o, n):
+            y_ps = psum.tile([P, W], F32, name="y_ps", tag="bank")
+            product(y_ps, ((dense_w_sb, hnew_sb),), o, n)
+            nc.scalar.copy(y_sb[o][:, n * W : (n + 1) * W], y_ps[:])
 
         transpose_ann(0)
         make_biases()
@@ -180,8 +179,10 @@ def tile_gatedgraphconvolution_b_kernel(
             for k in range(CB):
                 gru(n, k)
                 if k == 0 and n > 0:
-                    dense(n - 1)
-        dense(CHUNKS - 1)
+                    dense(0, n - 1)
+        dense(0, CHUNKS - 1)
+        for n in range(CHUNKS):
+            dense(1, n)
 
         for o in range(OB):
             nc.vector.tensor_tensor(

@@ -21,6 +21,8 @@ SIGMOID = mybir.ActivationFunctionType.Sigmoid
 TANH = mybir.ActivationFunctionType.Tanh
 IDENTITY = mybir.ActivationFunctionType.Identity
 
+Z, R, CAND = 0, 1, 2
+
 GC_COL = 0
 BX_COL = GC_COL + CB
 BH_COL = BX_COL + 3 * CB
@@ -37,9 +39,6 @@ def tile_gatedgraphconvolution_b_kernel(
         tc.tile_pool(name="work", bufs=3) as work,
         tc.psum_pool(name="psum", bufs=8) as psum,
     ):
-        offsets = held.tile([P, N // 16], U16, name="offsets")
-        nc.sync.dma_start(offsets[:], offs)
-
         bias_rows = held.tile([P, P], F32, name="bias_rows")
         nc.vector.memset(bias_rows[:], 0.0)
         for vector, col, blocks in (
@@ -54,16 +53,26 @@ def tile_gatedgraphconvolution_b_kernel(
         adj_sb = held.tile([P, Q * UB, T], BF16, name="adj_sb")
         ann_blocks = ann.rearrange("(k p) n -> p k n", p=P)
         adj_blocks = adj_t.flatten_outer_dims().rearrange("(b p) t -> p b t", p=P)
-        for n in range(CHUNKS):
+
+        def load_chunk(n):
             nc.sync.dma_start(ann_sb[:, :, n * W : (n + 1) * W], ann_blocks[:, :, n * W : (n + 1) * W])
             nc.scalar.dma_start(adj_sb[:, n * NB : (n + 1) * NB, :], adj_blocks[:, n * NB : (n + 1) * NB, :])
 
         gru_u_sb = held.tile([P, CB, 3 * C], BF16, name="gru_u_sb")
         gru_w_sb = held.tile([P, CB, 3 * C], BF16, name="gru_w_sb")
         dense_w_sb = held.tile([P, CB, O], BF16, name="dense_w_sb")
-        nc.sync.dma_start(gru_u_sb[:], gru_u.rearrange("(k p) m -> p k m", p=P))
-        nc.scalar.dma_start(gru_w_sb[:], gru_w.rearrange("(k p) m -> p k m", p=P))
+        gru_u_blocks = gru_u.rearrange("(k p) m -> p k m", p=P)
+        gru_w_blocks = gru_w.rearrange("(k p) m -> p k m", p=P)
+
+        load_chunk(0)
+        for gate in (R, CAND, Z):
+            nc.sync.dma_start(gru_u_sb[:, :, gate * C : (gate + 1) * C], gru_u_blocks[:, :, gate * C : (gate + 1) * C])
+            nc.scalar.dma_start(gru_w_sb[:, :, gate * C : (gate + 1) * C], gru_w_blocks[:, :, gate * C : (gate + 1) * C])
+        for n in range(1, CHUNKS):
+            load_chunk(n)
         nc.scalar.dma_start(dense_w_sb[:], dense_w.rearrange("(k p) m -> p k m", p=P))
+        offsets = held.tile([P, N // 16], U16, name="offsets")
+        nc.sync.dma_start(offsets[:], offs)
 
         windows = [held.tile([P, S], F32, name=f"window{o}") for o in range(OB)]
         nc.sync.dma_start(windows[0][:], base[0:P, :])
@@ -131,28 +140,28 @@ def tile_gatedgraphconvolution_b_kernel(
             from_state, from_msg = (gru_u_sb, ann_sb), (gru_w_sb, msg_sb)
 
             r_ps = psum.tile([P, W], F32, name="r_ps", tag="bank")
-            product(r_ps, (from_state, from_msg), CB + k, n)
+            product(r_ps, (from_state, from_msg), R * CB + k, n)
             r = work.tile([P, W], F32, name="r")
-            nc.scalar.activation(r[:], r_ps[:], SIGMOID, bias=gate_bias[:, CB + k : CB + k + 1])
+            nc.scalar.activation(r[:], r_ps[:], SIGMOID, bias=gate_bias[:, R * CB + k : R * CB + k + 1])
 
             ph_ps = psum.tile([P, W], F32, name="ph_ps", tag="bank")
-            product(ph_ps, (from_state,), 2 * CB + k, n)
+            product(ph_ps, (from_state,), CAND * CB + k, n)
             gated = work.tile([P, W], F32, name="gated")
-            bh_col = BH_COL + 2 * CB + k
+            bh_col = BH_COL + CAND * CB + k
             nc.vector.scalar_tensor_tensor(gated[:], ph_ps[:], bias_sb[:, bh_col : bh_col + 1], r[:], ADD, MULT)
 
             px_ps = psum.tile([P, W], F32, name="px_ps", tag="bank")
-            product(px_ps, (from_msg,), 2 * CB + k, n)
+            product(px_ps, (from_msg,), CAND * CB + k, n)
             pre = work.tile([P, W], F32, name="pre")
             nc.vector.tensor_tensor(pre[:], gated[:], px_ps[:], ADD)
             cand = work.tile([P, W], F32, name="cand")
-            bx_col = BX_COL + 2 * CB + k
+            bx_col = BX_COL + CAND * CB + k
             nc.scalar.activation(cand[:], pre[:], TANH, bias=bias_sb[:, bx_col : bx_col + 1])
 
             z_ps = psum.tile([P, W], F32, name="z_ps", tag="bank")
-            product(z_ps, (from_state, from_msg), k, n)
+            product(z_ps, (from_state, from_msg), Z * CB + k, n)
             z = work.tile([P, W], F32, name="z")
-            nc.scalar.activation(z[:], z_ps[:], SIGMOID, bias=gate_bias[:, k : k + 1])
+            nc.scalar.activation(z[:], z_ps[:], SIGMOID, bias=gate_bias[:, Z * CB + k : Z * CB + k + 1])
 
             diff = work.tile([P, W], F32, name="diff")
             nc.vector.tensor_tensor(diff[:], state, cand[:], SUBTRACT)
@@ -167,10 +176,7 @@ def tile_gatedgraphconvolution_b_kernel(
 
         transpose_ann(0)
         make_biases()
-        for n in range(CHUNKS):
-            if n + 1 < CHUNKS:
-                transpose_ann(n + 1)
-            adjacency(n)
+        adjacency(0)
 
         for o in range(OB):
             nc.vector.tensor_copy(dense_b_wide[o][:], bias_sb[:, DB_COL + o : DB_COL + o + 1].to_broadcast([P, N]))
@@ -180,6 +186,10 @@ def tile_gatedgraphconvolution_b_kernel(
                 gru(n, k)
                 if k == 0 and n > 0:
                     dense(0, n - 1)
+                if k == 1 and n + 1 < CHUNKS:
+                    transpose_ann(n + 1)
+                if k == 2 and n + 1 < CHUNKS:
+                    adjacency(n + 1)
         dense(0, CHUNKS - 1)
         for n in range(CHUNKS):
             dense(1, n)

@@ -39,16 +39,6 @@ def tile_gatedgraphconvolution_b_kernel(
         tc.tile_pool(name="work", bufs=3) as work,
         tc.psum_pool(name="psum", bufs=8) as psum,
     ):
-        bias_rows = held.tile([P, P], F32, name="bias_rows")
-        nc.vector.memset(bias_rows[:], 0.0)
-        for vector, col, blocks in (
-            (gc_bias, GC_COL, CB),
-            (gru_bx, BX_COL, 3 * CB),
-            (gru_bh, BH_COL, 3 * CB),
-            (dense_b, DB_COL, OB),
-        ):
-            nc.scalar.dma_start(bias_rows[col : col + blocks, :], vector.rearrange("(k p) one -> k (p one)", p=P))
-
         ann_sb = held.tile([P, CB, N], BF16, name="ann_sb")
         adj_sb = held.tile([P, Q * UB, T], BF16, name="adj_sb")
         ann_blocks = ann.rearrange("(k p) n -> p k n", p=P)
@@ -56,7 +46,7 @@ def tile_gatedgraphconvolution_b_kernel(
 
         def load_chunk(n):
             nc.sync.dma_start(ann_sb[:, :, n * W : (n + 1) * W], ann_blocks[:, :, n * W : (n + 1) * W])
-            nc.scalar.dma_start(adj_sb[:, n * NB : (n + 1) * NB, :], adj_blocks[:, n * NB : (n + 1) * NB, :])
+            nc.sync.dma_start(adj_sb[:, n * NB : (n + 1) * NB, :], adj_blocks[:, n * NB : (n + 1) * NB, :])
 
         gru_u_sb = held.tile([P, CB, 3 * C], BF16, name="gru_u_sb")
         gru_w_sb = held.tile([P, CB, 3 * C], BF16, name="gru_w_sb")
@@ -65,18 +55,27 @@ def tile_gatedgraphconvolution_b_kernel(
         gru_w_blocks = gru_w.rearrange("(k p) m -> p k m", p=P)
 
         load_chunk(0)
+        bias_rows = held.tile([P, P], F32, name="bias_rows")
+        nc.vector.memset(bias_rows[:], 0.0)
+        for vector, col, blocks in (
+            (gc_bias, GC_COL, CB),
+            (gru_bx, BX_COL, 3 * CB),
+            (gru_bh, BH_COL, 3 * CB),
+            (dense_b, DB_COL, OB),
+        ):
+            nc.sync.dma_start(bias_rows[col : col + blocks, :], vector.rearrange("(k p) one -> k (p one)", p=P))
         for gate in (R, CAND, Z):
             nc.sync.dma_start(gru_u_sb[:, :, gate * C : (gate + 1) * C], gru_u_blocks[:, :, gate * C : (gate + 1) * C])
-            nc.scalar.dma_start(gru_w_sb[:, :, gate * C : (gate + 1) * C], gru_w_blocks[:, :, gate * C : (gate + 1) * C])
+            nc.sync.dma_start(gru_w_sb[:, :, gate * C : (gate + 1) * C], gru_w_blocks[:, :, gate * C : (gate + 1) * C])
         for n in range(1, CHUNKS):
             load_chunk(n)
-        nc.scalar.dma_start(dense_w_sb[:], dense_w.rearrange("(k p) m -> p k m", p=P))
+        nc.sync.dma_start(dense_w_sb[:], dense_w.rearrange("(k p) m -> p k m", p=P))
         offsets = held.tile([P, N // 16], U16, name="offsets")
         nc.sync.dma_start(offsets[:], offs)
 
         windows = [held.tile([P, S], F32, name=f"window{o}") for o in range(OB)]
         nc.sync.dma_start(windows[0][:], base[0:P, :])
-        nc.scalar.dma_start(windows[1][:], base[P : 2 * P, :])
+        nc.sync.dma_start(windows[1][:], base[P : 2 * P, :])
 
         ident_bf = held.tile([P, P], BF16, name="ident_bf")
         make_identity(nc, ident_bf[:])

@@ -183,15 +183,14 @@ def tile_gatedgraphconvolution_b_kernel(
         for n in range(CHUNKS):
             for k in range(CB):
                 gru(n, k)
-                if k == 0 and n > 0:
-                    dense(0, n - 1)
                 if k == 1 and n + 1 < CHUNKS:
                     transpose_ann(n + 1)
                 if k == 2 and n + 1 < CHUNKS:
                     adjacency(n + 1)
-        dense(0, CHUNKS - 1)
-        for n in range(CHUNKS):
-            dense(1, n)
+
+        for o in range(OB):
+            for n in range(CHUNKS):
+                dense(o, n)
 
         for o in range(OB):
             nc.vector.tensor_tensor(

@@ -92,9 +92,15 @@ def tile_gatedgraphconvolution_b_kernel(
 
         def transpose_ann(n):
             for b in range(n * NB, (n + 1) * NB):
-                flipped = psum.tile([P, C], BF16, name="flipped", tag="bank")
+                flipped = psum.tile([P, C], F32, name="flipped", tag="bank")
                 for k in range(CB):
-                    nc.tensor.transpose(flipped[:, k * P : (k + 1) * P], ann_sb[:, k, b * P : (b + 1) * P], ident_bf[:])
+                    nc.tensor.matmul(
+                        flipped[:, k * P : (k + 1) * P],
+                        ann_sb[:, k, b * P : (b + 1) * P],
+                        ident_bf[:],
+                        start=True,
+                        stop=True,
+                    )
                 nc.vector.tensor_copy(ann_t_sb[:, b, :], flipped[:])
 
         def make_biases():

@@ -36,6 +36,8 @@ def tile_gatedgraphconvolution_b_kernel(
     nc = tc.nc
     with (
         tc.tile_pool(name="held", bufs=1) as held,
+        tc.tile_pool(name="flip", bufs=2) as flip,
+        tc.tile_pool(name="kept", bufs=CB) as kept,
         tc.tile_pool(name="work", bufs=3) as work,
         tc.psum_pool(name="psum", bufs=8) as psum,
     ):
@@ -54,7 +56,10 @@ def tile_gatedgraphconvolution_b_kernel(
         gru_u_blocks = gru_u.rearrange("(k p) m -> p k m", p=P)
         gru_w_blocks = gru_w.rearrange("(k p) m -> p k m", p=P)
 
-        load_chunk(0)
+        for k in range(CB):
+            nc.sync.dma_start(ann_sb[:, k, 0:W], ann_blocks[:, k, 0:W])
+            nc.sync.dma_start(gru_u_sb[:, k, R * C : (R + 1) * C], gru_u_blocks[:, k, R * C : (R + 1) * C])
+        nc.sync.dma_start(adj_sb[:, 0:NB, :], adj_blocks[:, 0:NB, :])
         bias_rows = held.tile([P, P], F32, name="bias_rows")
         nc.vector.memset(bias_rows[:], 0.0)
         for vector, col, blocks in (
@@ -64,7 +69,8 @@ def tile_gatedgraphconvolution_b_kernel(
             (dense_b, DB_COL, OB),
         ):
             nc.sync.dma_start(bias_rows[col : col + blocks, :], vector.rearrange("(k p) one -> k (p one)", p=P))
-        for gate in (R, CAND, Z):
+        nc.sync.dma_start(gru_w_sb[:, :, R * C : (R + 1) * C], gru_w_blocks[:, :, R * C : (R + 1) * C])
+        for gate in (CAND, Z):
             nc.sync.dma_start(gru_u_sb[:, :, gate * C : (gate + 1) * C], gru_u_blocks[:, :, gate * C : (gate + 1) * C])
             nc.sync.dma_start(gru_w_sb[:, :, gate * C : (gate + 1) * C], gru_w_blocks[:, :, gate * C : (gate + 1) * C])
         for n in range(1, CHUNKS):
@@ -72,36 +78,21 @@ def tile_gatedgraphconvolution_b_kernel(
         nc.sync.dma_start(dense_w_sb[:], dense_w.rearrange("(k p) m -> p k m", p=P))
         offsets = held.tile([P, N // 16], U16, name="offsets")
         nc.sync.dma_start(offsets[:], offs)
-
         windows = [held.tile([P, S], F32, name=f"window{o}") for o in range(OB)]
-        nc.sync.dma_start(windows[0][:], base[0:P, :])
-        nc.sync.dma_start(windows[1][:], base[P : 2 * P, :])
+        for o in range(OB):
+            nc.sync.dma_start(windows[o][:], base[o * P : (o + 1) * P, :])
 
         ident_bf = held.tile([P, P], BF16, name="ident_bf")
         make_identity(nc, ident_bf[:])
         ident_f32 = held.tile([P, P], F32, name="ident_f32")
         nc.vector.tensor_copy(ident_f32[:], ident_bf[:])
 
-        ann_t_sb = held.tile([P, N // P, C], BF16, name="ann_t_sb")
         msg_sb = held.tile([P, CB, N], BF16, name="msg_sb")
         hnew_sb = held.tile([P, CB, N], BF16, name="hnew_sb")
         y_sb = [held.tile([P, N], F32, name=f"y_sb{o}") for o in range(OB)]
         bias_sb = held.tile([P, BIAS_COLS], F32, name="bias_sb")
         gate_bias = held.tile([P, 2 * CB], F32, name="gate_bias")
         dense_b_wide = [held.tile([P, N], F32, name=f"dense_b_wide{o}") for o in range(OB)]
-
-        def transpose_ann(n):
-            for b in range(n * NB, (n + 1) * NB):
-                flipped = psum.tile([P, C], F32, name="flipped", tag="bank")
-                for k in range(CB):
-                    nc.tensor.matmul(
-                        flipped[:, k * P : (k + 1) * P],
-                        ann_sb[:, k, b * P : (b + 1) * P],
-                        ident_bf[:],
-                        start=True,
-                        stop=True,
-                    )
-                nc.vector.tensor_copy(ann_t_sb[:, b, :], flipped[:])
 
         def make_biases():
             columns = psum.tile([P, P], F32, name="columns", tag="bank")
@@ -111,16 +102,26 @@ def tile_gatedgraphconvolution_b_kernel(
                 gate_bias[:], bias_sb[:, BX_COL : BX_COL + 2 * CB], bias_sb[:, BH_COL : BH_COL + 2 * CB], ADD
             )
 
-        def adjacency(n):
+        def new_ann_t():
+            return flip.tile([P, CB, NB, P], BF16, name="ann_t")
+
+        def new_flips():
+            return psum.tile([P, NB, P], BF16, name="flips", tag="bank")
+
+        def flip_block(flips, n, k, b):
+            lo = n * W + b * P
+            nc.tensor.transpose(flips[:, b, :], ann_sb[:, k, lo : lo + P], ident_bf[:])
+
+        def adjacency(n, ann_t):
             for k in range(CB):
                 msg_ps = psum.tile([P, W], F32, name="msg_ps", tag="bank")
                 for g in range(GRAPHS):
                     for u in range(UB):
-                        b = (n * GRAPHS + g) * UB + u
+                        b = g * UB + u
                         nc.tensor.matmul(
                             msg_ps[:, g * T : (g + 1) * T],
-                            ann_t_sb[:, b, k * P : (k + 1) * P],
-                            adj_sb[:, b, :],
+                            ann_t[:, k, b, :],
+                            adj_sb[:, n * NB + b, :],
                             start=(u == 0),
                             stop=(u == UB - 1),
                         )
@@ -128,75 +129,115 @@ def tile_gatedgraphconvolution_b_kernel(
                     msg_sb[:, k, n * W : (n + 1) * W], msg_ps[:], IDENTITY, bias=bias_sb[:, GC_COL + k : GC_COL + k + 1]
                 )
 
-        def product(bank, terms, m, n):
-            last = len(terms) * CB - 1
-            for i, (weights, moving) in enumerate(terms):
-                for k in range(CB):
-                    nc.tensor.matmul(
-                        bank[:],
-                        weights[:, k, m * P : (m + 1) * P],
-                        moving[:, k, n * W : (n + 1) * W],
-                        start=(i * CB + k == 0),
-                        stop=(i * CB + k == last),
-                    )
+        from_state, from_msg = (gru_u_sb, ann_sb), (gru_w_sb, msg_sb)
 
-        def gru(n, k):
-            state = ann_sb[:, k, n * W : (n + 1) * W]
-            from_state, from_msg = (gru_u_sb, ann_sb), (gru_w_sb, msg_sb)
+        def product_term(bank, term, k, m, n, start, stop):
+            weights, moving = term
+            nc.tensor.matmul(
+                bank[:],
+                weights[:, k, m * P : (m + 1) * P],
+                moving[:, k, n * W : (n + 1) * W],
+                start=start,
+                stop=stop,
+            )
 
-            r_ps = psum.tile([P, W], F32, name="r_ps", tag="bank")
-            product(r_ps, (from_state, from_msg), R * CB + k, n)
-            r = work.tile([P, W], F32, name="r")
-            nc.scalar.activation(r[:], r_ps[:], SIGMOID, bias=gate_bias[:, R * CB + k : R * CB + k + 1])
+        def product(bank, term, m, n, start=True, stop=True, beside=None):
+            for k in range(CB):
+                product_term(bank, term, k, m, n, start and k == 0, stop and k == CB - 1)
+                if beside is not None:
+                    beside(k)
 
+        def sigmoid(gate_ps, k, rows, name):
+            opened = kept.tile([P, W], F32, name=name)
+            nc.scalar.activation(opened[:], gate_ps[:], SIGMOID, bias=gate_bias[:, rows * CB + k : rows * CB + k + 1])
+            return opened
+
+        def gate(n, k, rows, name):
+            gate_ps = psum.tile([P, W], F32, name="gate_ps", tag="bank")
+            product(gate_ps, from_state, rows * CB + k, n, stop=False)
+            product(gate_ps, from_msg, rows * CB + k, n, start=False)
+            return sigmoid(gate_ps, k, rows, name)
+
+        def candidate(n, k, r, next_ann_t):
             ph_ps = psum.tile([P, W], F32, name="ph_ps", tag="bank")
-            product(ph_ps, (from_state,), CAND * CB + k, n)
+            if next_ann_t is None:
+                product(ph_ps, from_state, CAND * CB + k, n)
+            else:
+                flips = new_flips()
+                product(ph_ps, from_state, CAND * CB + k, n, beside=lambda b: flip_block(flips, n + 1, k, b))
+                nc.vector.tensor_copy(next_ann_t[:, k, :, :], flips[:])
             gated = work.tile([P, W], F32, name="gated")
             bh_col = BH_COL + CAND * CB + k
             nc.vector.scalar_tensor_tensor(gated[:], ph_ps[:], bias_sb[:, bh_col : bh_col + 1], r[:], ADD, MULT)
 
             px_ps = psum.tile([P, W], F32, name="px_ps", tag="bank")
-            product(px_ps, (from_msg,), CAND * CB + k, n)
+            product(px_ps, from_msg, CAND * CB + k, n)
             pre = work.tile([P, W], F32, name="pre")
             nc.vector.tensor_tensor(pre[:], gated[:], px_ps[:], ADD)
             cand = work.tile([P, W], F32, name="cand")
             bx_col = BX_COL + CAND * CB + k
             nc.scalar.activation(cand[:], pre[:], TANH, bias=bias_sb[:, bx_col : bx_col + 1])
+            return cand
 
-            z_ps = psum.tile([P, W], F32, name="z_ps", tag="bank")
-            product(z_ps, (from_state, from_msg), Z * CB + k, n)
-            z = work.tile([P, W], F32, name="z")
-            nc.scalar.activation(z[:], z_ps[:], SIGMOID, bias=gate_bias[:, Z * CB + k : Z * CB + k + 1])
-
+        def blend(n, k, z, cand):
             diff = work.tile([P, W], F32, name="diff")
-            nc.vector.tensor_tensor(diff[:], state, cand[:], SUBTRACT)
-            kept = work.tile([P, W], F32, name="kept")
-            nc.vector.tensor_tensor(kept[:], z[:], diff[:], MULT)
-            nc.vector.tensor_tensor(hnew_sb[:, k, n * W : (n + 1) * W], kept[:], cand[:], ADD)
+            nc.vector.tensor_tensor(diff[:], ann_sb[:, k, n * W : (n + 1) * W], cand[:], SUBTRACT)
+            step = work.tile([P, W], F32, name="step")
+            nc.vector.tensor_tensor(step[:], z[:], diff[:], MULT)
+            nc.vector.tensor_tensor(hnew_sb[:, k, n * W : (n + 1) * W], step[:], cand[:], ADD)
 
-        def dense(o, n):
-            y_ps = psum.tile([P, W], F32, name="y_ps", tag="bank")
-            product(y_ps, ((dense_w_sb, hnew_sb),), o, n)
-            nc.scalar.copy(y_sb[o][:, n * W : (n + 1) * W], y_ps[:])
+        def dense(o, n, copies):
+            width = W // len(copies)
+            for i, copy_out in enumerate(copies):
+                lo = n * W + i * width
+                y_ps = psum.tile([P, width], F32, name="y_ps", tag="bank")
+                for k in range(CB):
+                    nc.tensor.matmul(
+                        y_ps[:],
+                        dense_w_sb[:, k, o * P : (o + 1) * P],
+                        hnew_sb[:, k, lo : lo + width],
+                        start=(k == 0),
+                        stop=(k == CB - 1),
+                    )
+                copy_out(y_sb[o][:, lo : lo + width], y_ps[:])
 
-        transpose_ann(0)
-        make_biases()
-        adjacency(0)
+        first_r_ps = [psum.tile([P, W], F32, name=f"first_r_ps{m}", tag="bank") for m in range(CB)]
+        ann_t = new_ann_t()
+        for k in range(CB):
+            if k == CB - 1:
+                make_biases()
+            flips = new_flips()
+            for m, b in zip(range(CB), range(NB)):
+                product_term(first_r_ps[m], from_state, k, R * CB + m, 0, start=(k == 0), stop=False)
+                flip_block(flips, 0, k, b)
+            nc.vector.tensor_copy(ann_t[:, k, :, :], flips[:])
+
+        adjacency(0, ann_t)
+
+        for k in range(CB):
+            for m in range(CB):
+                product_term(first_r_ps[m], from_msg, k, R * CB + m, 0, start=False, stop=(k == CB - 1))
+        first_r = [sigmoid(first_r_ps[m], m, R, "r") for m in range(CB)]
 
         for o in range(OB):
             nc.vector.tensor_copy(dense_b_wide[o][:], bias_sb[:, DB_COL + o : DB_COL + o + 1].to_broadcast([P, N]))
 
         for n in range(CHUNKS):
+            next_ann_t = new_ann_t() if n + 1 < CHUNKS else None
             for k in range(CB):
-                gru(n, k)
-                if k == 1 and n + 1 < CHUNKS:
-                    transpose_ann(n + 1)
-                if k == 2 and n + 1 < CHUNKS:
-                    adjacency(n + 1)
+                r = first_r[k] if n == 0 else gate(n, k, R, "r")
+                cand = candidate(n, k, r, next_ann_t)
+                z = gate(n, k, Z, "z")
+                blend(n, k, z, cand)
+            if next_ann_t is not None:
+                adjacency(n + 1, next_ann_t)
 
         for o in range(OB):
             for n in range(CHUNKS):
-                dense(o, n)
+                if o == 0 and n == CHUNKS - 1:
+                    dense(o, n, (nc.scalar.copy, nc.vector.tensor_copy))
+                else:
+                    dense(o, n, (nc.scalar.copy,))
 
         for o in range(OB):
             nc.vector.tensor_tensor(

@@ -186,20 +186,17 @@ def tile_gatedgraphconvolution_b_kernel(
             nc.vector.tensor_tensor(step[:], z[:], diff[:], MULT)
             nc.vector.tensor_tensor(hnew_sb[:, k, n * W : (n + 1) * W], step[:], cand[:], ADD)
 
-        def dense(o, n, copies):
-            width = W // len(copies)
-            for i, copy_out in enumerate(copies):
-                lo = n * W + i * width
-                y_ps = psum.tile([P, width], F32, name="y_ps", tag="bank")
-                for k in range(CB):
-                    nc.tensor.matmul(
-                        y_ps[:],
-                        dense_w_sb[:, k, o * P : (o + 1) * P],
-                        hnew_sb[:, k, lo : lo + width],
-                        start=(k == 0),
-                        stop=(k == CB - 1),
-                    )
-                copy_out(y_sb[o][:, lo : lo + width], y_ps[:])
+        def dense(o, lo, width, copy_out):
+            y_ps = psum.tile([P, width], F32, name="y_ps", tag="bank")
+            for k in range(CB):
+                nc.tensor.matmul(
+                    y_ps[:],
+                    dense_w_sb[:, k, o * P : (o + 1) * P],
+                    hnew_sb[:, k, lo : lo + width],
+                    start=(k == 0),
+                    stop=(k == CB - 1),
+                )
+            copy_out(y_sb[o][:, lo : lo + width], y_ps[:])
 
         first_r_ps = [psum.tile([P, W], F32, name=f"first_r_ps{m}", tag="bank") for m in range(CB)]
         ann_t = new_ann_t()
@@ -219,9 +216,6 @@ def tile_gatedgraphconvolution_b_kernel(
                 product_term(first_r_ps[m], from_msg, k, R * CB + m, 0, start=False, stop=(k == CB - 1))
         first_r = [sigmoid(first_r_ps[m], m, R, "r") for m in range(CB)]
 
-        for o in range(OB):
-            nc.vector.tensor_copy(dense_b_wide[o][:], bias_sb[:, DB_COL + o : DB_COL + o + 1].to_broadcast([P, N]))
-
         for n in range(CHUNKS):
             next_ann_t = new_ann_t() if n + 1 < CHUNKS else None
             for k in range(CB):
@@ -231,13 +225,18 @@ def tile_gatedgraphconvolution_b_kernel(
                 blend(n, k, z, cand)
             if next_ann_t is not None:
                 adjacency(n + 1, next_ann_t)
+            for o in range(OB):
+                nc.vector.tensor_copy(
+                    dense_b_wide[o][:, n * W : (n + 1) * W],
+                    bias_sb[:, DB_COL + o : DB_COL + o + 1].to_broadcast([P, W]),
+                )
 
-        for o in range(OB):
-            for n in range(CHUNKS):
-                if o == 0 and n == CHUNKS - 1:
-                    dense(o, n, (nc.scalar.copy, nc.vector.tensor_copy))
-                else:
-                    dense(o, n, (nc.scalar.copy,))
+        head = N - W // 4
+        for lo in range(0, N, W):
+            dense(0, lo, min(W, head - lo), nc.scalar.copy)
+        dense(0, head, N - head, nc.vector.tensor_copy)
+        for lo in range(0, N, W):
+            dense(1, lo, W, nc.scalar.copy)
 
         for o in range(OB):
             nc.vector.tensor_tensor(

import concourse.mybir as mybir
from concourse.masks import make_identity

P = 128
Q, T = 8, 256
C, O, S = 512, 256, 4096
N = Q * T
CB = C // P
OB = O // P
W = 512
CHUNKS = N // W
GRAPHS = W // T
UB = T // P
NB = W // P

FLOPS = 2 * (Q * C * T * T + 2 * C * 3 * C * N + C * O * N)

BF16, F32, U16 = mybir.dt.bfloat16, mybir.dt.float32, mybir.dt.uint16
ADD, MULT, SUBTRACT = mybir.AluOpType.add, mybir.AluOpType.mult, mybir.AluOpType.subtract
SIGMOID = mybir.ActivationFunctionType.Sigmoid
TANH = mybir.ActivationFunctionType.Tanh
IDENTITY = mybir.ActivationFunctionType.Identity

Z, R, CAND = 0, 1, 2

GC_COL = 0
BX_COL = GC_COL + CB
BH_COL = BX_COL + 3 * CB
DB_COL = BH_COL + 3 * CB
BIAS_COLS = DB_COL + OB


def tile_gatedgraphconvolution_b_kernel(
    tc, base, adj_t, ann, gc_bias, gru_w, gru_u, gru_bx, gru_bh, dense_w, dense_b, offs, out
):
    nc = tc.nc
    with (
        tc.tile_pool(name="held", bufs=1) as held,
        tc.tile_pool(name="flip", bufs=2) as flip,
        tc.tile_pool(name="kept", bufs=CB) as kept,
        tc.tile_pool(name="work", bufs=3) as work,
        tc.psum_pool(name="psum", bufs=8) as psum,
    ):
        ann_sb = held.tile([P, CB, N], BF16, name="ann_sb")
        adj_sb = held.tile([P, Q * UB, T], BF16, name="adj_sb")
        ann_blocks = ann.rearrange("(k p) n -> p k n", p=P)
        adj_blocks = adj_t.flatten_outer_dims().rearrange("(b p) t -> p b t", p=P)

        def load_chunk(n):
            nc.sync.dma_start(ann_sb[:, :, n * W : (n + 1) * W], ann_blocks[:, :, n * W : (n + 1) * W])
            nc.sync.dma_start(adj_sb[:, n * NB : (n + 1) * NB, :], adj_blocks[:, n * NB : (n + 1) * NB, :])

        gru_u_sb = held.tile([P, CB, 3 * C], BF16, name="gru_u_sb")
        gru_w_sb = held.tile([P, CB, 3 * C], BF16, name="gru_w_sb")
        dense_w_sb = held.tile([P, CB, O], BF16, name="dense_w_sb")
        gru_u_blocks = gru_u.rearrange("(k p) m -> p k m", p=P)
        gru_w_blocks = gru_w.rearrange("(k p) m -> p k m", p=P)

        for k in range(CB):
            nc.sync.dma_start(ann_sb[:, k, 0:W], ann_blocks[:, k, 0:W])
            nc.sync.dma_start(gru_u_sb[:, k, R * C : (R + 1) * C], gru_u_blocks[:, k, R * C : (R + 1) * C])
        nc.sync.dma_start(adj_sb[:, 0:NB, :], adj_blocks[:, 0:NB, :])
        bias_rows = held.tile([P, P], F32, name="bias_rows")
        nc.vector.memset(bias_rows[:], 0.0)
        for vector, col, blocks in (
            (gc_bias, GC_COL, CB),
            (gru_bx, BX_COL, 3 * CB),
            (gru_bh, BH_COL, 3 * CB),
            (dense_b, DB_COL, OB),
        ):
            nc.sync.dma_start(bias_rows[col : col + blocks, :], vector.rearrange("(k p) one -> k (p one)", p=P))
        nc.sync.dma_start(gru_w_sb[:, :, R * C : (R + 1) * C], gru_w_blocks[:, :, R * C : (R + 1) * C])
        for gate in (CAND, Z):
            nc.sync.dma_start(gru_u_sb[:, :, gate * C : (gate + 1) * C], gru_u_blocks[:, :, gate * C : (gate + 1) * C])
            nc.sync.dma_start(gru_w_sb[:, :, gate * C : (gate + 1) * C], gru_w_blocks[:, :, gate * C : (gate + 1) * C])
        for n in range(1, CHUNKS):
            load_chunk(n)
        nc.sync.dma_start(dense_w_sb[:], dense_w.rearrange("(k p) m -> p k m", p=P))
        offsets = held.tile([P, N // 16], U16, name="offsets")
        nc.sync.dma_start(offsets[:], offs)
        windows = [held.tile([P, S], F32, name=f"window{o}") for o in range(OB)]
        for o in range(OB):
            nc.sync.dma_start(windows[o][:], base[o * P : (o + 1) * P, :])

        ident_bf = held.tile([P, P], BF16, name="ident_bf")
        make_identity(nc, ident_bf[:])
        ident_f32 = held.tile([P, P], F32, name="ident_f32")
        nc.vector.tensor_copy(ident_f32[:], ident_bf[:])

        msg_sb = held.tile([P, CB, N], BF16, name="msg_sb")
        hnew_sb = held.tile([P, CB, N], BF16, name="hnew_sb")
        y_sb = [held.tile([P, N], F32, name=f"y_sb{o}") for o in range(OB)]
        bias_sb = held.tile([P, BIAS_COLS], F32, name="bias_sb")
        gate_bias = held.tile([P, 2 * CB], F32, name="gate_bias")
        dense_b_wide = [held.tile([P, N], F32, name=f"dense_b_wide{o}") for o in range(OB)]

        def make_biases():
            columns = psum.tile([P, P], F32, name="columns", tag="bank")
            nc.tensor.transpose(columns[:], bias_rows[:], ident_f32[:])
            nc.vector.tensor_copy(bias_sb[:], columns[:, 0:BIAS_COLS])
            nc.vector.tensor_tensor(
                gate_bias[:], bias_sb[:, BX_COL : BX_COL + 2 * CB], bias_sb[:, BH_COL : BH_COL + 2 * CB], ADD
            )

        def new_ann_t():
            return flip.tile([P, CB, NB, P], BF16, name="ann_t")

        def new_flips():
            return psum.tile([P, NB, P], BF16, name="flips", tag="bank")

        def flip_block(flips, n, k, b):
            lo = n * W + b * P
            nc.tensor.transpose(flips[:, b, :], ann_sb[:, k, lo : lo + P], ident_bf[:])

        def adjacency(n, ann_t):
            for k in range(CB):
                msg_ps = psum.tile([P, W], F32, name="msg_ps", tag="bank")
                for g in range(GRAPHS):
                    for u in range(UB):
                        b = g * UB + u
                        nc.tensor.matmul(
                            msg_ps[:, g * T : (g + 1) * T],
                            ann_t[:, k, b, :],
                            adj_sb[:, n * NB + b, :],
                            start=(u == 0),
                            stop=(u == UB - 1),
                        )
                nc.scalar.activation(
                    msg_sb[:, k, n * W : (n + 1) * W], msg_ps[:], IDENTITY, bias=bias_sb[:, GC_COL + k : GC_COL + k + 1]
                )

        from_state, from_msg = (gru_u_sb, ann_sb), (gru_w_sb, msg_sb)

        def product_term(bank, term, k, m, n, start, stop):
            weights, moving = term
            nc.tensor.matmul(
                bank[:],
                weights[:, k, m * P : (m + 1) * P],
                moving[:, k, n * W : (n + 1) * W],
                start=start,
                stop=stop,
            )

        def product(bank, term, m, n, start=True, stop=True, beside=None):
            for k in range(CB):
                product_term(bank, term, k, m, n, start and k == 0, stop and k == CB - 1)
                if beside is not None:
                    beside(k)

        def sigmoid(gate_ps, k, rows, name):
            opened = kept.tile([P, W], F32, name=name)
            nc.scalar.activation(opened[:], gate_ps[:], SIGMOID, bias=gate_bias[:, rows * CB + k : rows * CB + k + 1])
            return opened

        def gate(n, k, rows, name):
            gate_ps = psum.tile([P, W], F32, name="gate_ps", tag="bank")
            product(gate_ps, from_state, rows * CB + k, n, stop=False)
            product(gate_ps, from_msg, rows * CB + k, n, start=False)
            return sigmoid(gate_ps, k, rows, name)

        def candidate(n, k, r, next_ann_t):
            ph_ps = psum.tile([P, W], F32, name="ph_ps", tag="bank")
            if next_ann_t is None:
                product(ph_ps, from_state, CAND * CB + k, n)
            else:
                flips = new_flips()
                product(ph_ps, from_state, CAND * CB + k, n, beside=lambda b: flip_block(flips, n + 1, k, b))
                nc.vector.tensor_copy(next_ann_t[:, k, :, :], flips[:])
            gated = work.tile([P, W], F32, name="gated")
            bh_col = BH_COL + CAND * CB + k
            nc.vector.scalar_tensor_tensor(gated[:], ph_ps[:], bias_sb[:, bh_col : bh_col + 1], r[:], ADD, MULT)

            px_ps = psum.tile([P, W], F32, name="px_ps", tag="bank")
            product(px_ps, from_msg, CAND * CB + k, n)
            pre = work.tile([P, W], F32, name="pre")
            nc.vector.tensor_tensor(pre[:], gated[:], px_ps[:], ADD)
            cand = work.tile([P, W], F32, name="cand")
            bx_col = BX_COL + CAND * CB + k
            nc.scalar.activation(cand[:], pre[:], TANH, bias=bias_sb[:, bx_col : bx_col + 1])
            return cand

        def blend(n, k, z, cand):
            diff = work.tile([P, W], F32, name="diff")
            nc.vector.tensor_tensor(diff[:], ann_sb[:, k, n * W : (n + 1) * W], cand[:], SUBTRACT)
            step = work.tile([P, W], F32, name="step")
            nc.vector.tensor_tensor(step[:], z[:], diff[:], MULT)
            nc.vector.tensor_tensor(hnew_sb[:, k, n * W : (n + 1) * W], step[:], cand[:], ADD)

        def dense(o, lo, width, copy_out):
            y_ps = psum.tile([P, width], F32, name="y_ps", tag="bank")
            for k in range(CB):
                nc.tensor.matmul(
                    y_ps[:],
                    dense_w_sb[:, k, o * P : (o + 1) * P],
                    hnew_sb[:, k, lo : lo + width],
                    start=(k == 0),
                    stop=(k == CB - 1),
                )
            copy_out(y_sb[o][:, lo : lo + width], y_ps[:])

        first_r_ps = [psum.tile([P, W], F32, name=f"first_r_ps{m}", tag="bank") for m in range(CB)]
        ann_t = new_ann_t()
        for k in range(CB):
            if k == CB - 1:
                make_biases()
            flips = new_flips()
            for m, b in zip(range(CB), range(NB)):
                product_term(first_r_ps[m], from_state, k, R * CB + m, 0, start=(k == 0), stop=False)
                flip_block(flips, 0, k, b)
            nc.vector.tensor_copy(ann_t[:, k, :, :], flips[:])

        adjacency(0, ann_t)

        for k in range(CB):
            for m in range(CB):
                product_term(first_r_ps[m], from_msg, k, R * CB + m, 0, start=False, stop=(k == CB - 1))
        first_r = [sigmoid(first_r_ps[m], m, R, "r") for m in range(CB)]

        for n in range(CHUNKS):
            next_ann_t = new_ann_t() if n + 1 < CHUNKS else None
            for k in range(CB):
                r = first_r[k] if n == 0 else gate(n, k, R, "r")
                cand = candidate(n, k, r, next_ann_t)
                z = gate(n, k, Z, "z")
                blend(n, k, z, cand)
            if next_ann_t is not None:
                adjacency(n + 1, next_ann_t)
            for o in range(OB):
                nc.vector.tensor_copy(
                    dense_b_wide[o][:, n * W : (n + 1) * W],
                    bias_sb[:, DB_COL + o : DB_COL + o + 1].to_broadcast([P, W]),
                )

        head = N - W // 4
        for lo in range(0, N, W):
            dense(0, lo, min(W, head - lo), nc.scalar.copy)
        dense(0, head, N - head, nc.vector.tensor_copy)
        for lo in range(0, N, W):
            dense(1, lo, W, nc.scalar.copy)

        for o in range(OB):
            nc.vector.tensor_tensor(
                windows[o][:].indirect(offsets[:]),
                y_sb[o][:],
                dense_b_wide[o][:],
                ADD,
            )
            nc.sync.dma_start(out[o * P : (o + 1) * P, :], windows[o][:])
